import numpy as np
import ml_dtypes


def mxq(x, axis, fmt="e4m3"):
    dtype, down = {"e4m3": (ml_dtypes.float8_e4m3fn, 7), "e5m2": (ml_dtypes.float8_e5m2, 14)}[fmt]
    v = np.moveaxis(np.asarray(x, np.float32).astype(ml_dtypes.bfloat16).astype(np.float64), axis, -1)
    blocks = v.reshape(v.shape[:-1] + (-1, 32))
    amax = np.abs(blocks).max(-1, keepdims=True)
    byte = np.maximum(np.where(amax > 0, np.frexp(amax)[1] - 1 + 127, 0) - down, 1)
    scale = np.exp2(byte - 127.0)
    codes = (blocks / scale).astype(np.float32).astype(dtype).astype(np.float64)
    return np.moveaxis((codes * scale).reshape(v.shape), -1, axis)


WIDE = False


def mx_kscale(k):
    if not WIDE:
        return np.ones(k)
    levels = np.array([20, -20, 10, -10, 0])
    a = np.random.permutation(np.resize(levels, k // 512 * 4)).reshape(k // 512, 4)
    idx = np.arange(k)
    return np.exp2(a[idx // 512, idx % 128 // 32])


BF16 = ml_dtypes.bfloat16


def bf(x):
    return np.asarray(x, np.float32).astype(BF16)


def f64(x):
    return np.asarray(x).astype(np.float64)


B, S, D, O = 4, 2048, 1024, 512
T = B * S
SUB_SIZE = 32
STEP = 2.0 ** -7


def draw_weight():
    n = O * D // SUB_SIZE
    q = np.random.randint(0, 16, (n, SUB_SIZE))
    r = np.arange(n)
    q[r, np.random.randint(0, SUB_SIZE // 2, n)] = 0
    q[r, SUB_SIZE // 2 + np.random.randint(0, SUB_SIZE // 2, n)] = 15
    return ((q - 8) * STEP).reshape(O, D)


def setup_inputs():
    s = mx_kscale(T).reshape(B, S, 1)
    x = np.random.standard_normal((B, S, D)) * s
    weight = draw_weight()
    bias = np.random.standard_normal(O)
    g = np.random.standard_normal((B, S, O)) * np.exp2(np.random.randint(-12, 1, (B, S, 1))) * 0.25 / s
    return {"x": bf(x), "weight": bf(weight), "bias": bf(bias), "grad_out": bf(g)}


def reference(x, weight, bias, grad_out):
    xt = f64(x).reshape(T, D)
    gt = f64(grad_out).reshape(T, O)
    return mxq(gt, 0, "e5m2").T @ mxq(xt, 0, "e4m3")

@@ -1,0 +1,133 @@
+from contextlib import ExitStack
+
+import concourse.mybir as mybir
+
+BF16 = mybir.dt.bfloat16
+F32 = mybir.dt.float32
+U32 = mybir.dt.uint32
+U8 = mybir.dt.uint8
+E4M3X4 = mybir.dt.float8_e4m3fn_x4
+E5M2X4 = mybir.dt.float8_e5m2_x4
+
+P = 128
+PACK = 4
+K_PASS = P * PACK
+T = 4 * 2048
+D = 1024
+O = 512
+N_TILE = 512
+CHUNKS = T // K_PASS
+M_TILES = O // P
+N_TILES = D // N_TILE
+
+FLOPS = 2 * T * O * D
+BYTES = 2 * T * D + 2 * T * O + 4 * O * D
+
+RAW_BUFS = 8
+SX = 768
+RUN = 4
+
+
+def tile_fakequantlinear_t_kernel(tc, x, weight, bias, grad_out, out):
+    nc = tc.nc
+    xf = x.rearrange("b s d -> (b s) d")
+    gf = grad_out.rearrange("b s o -> (b s) o")
+
+    with ExitStack() as ctx:
+        raw = ctx.enter_context(tc.tile_pool(name="raw", bufs=RAW_BUFS))
+        grp = ctx.enter_context(tc.tile_pool(name="grp", bufs=3))
+        cod = ctx.enter_context(tc.tile_pool(name="cod", bufs=3))
+        res = ctx.enter_context(tc.tile_pool(name="res", bufs=M_TILES * N_TILES))
+        psum = ctx.enter_context(tc.psum_pool(name="psum", bufs=1))
+        ctx.enter_context(tc.manual_schedule())
+
+        acc = {}
+        for m in range(M_TILES):
+            for n in range(N_TILES):
+                acc[(m, n)] = psum.tile([P, N_TILE], F32, name="acc%d%d" % (m, n))
+
+        x_raw = {}
+        g_raw = {}
+        x_grp = {}
+        g_grp = {}
+        x_cod = {}
+        g_cod = {}
+
+        def load(c):
+            rows = slice(c * K_PASS, (c + 1) * K_PASS)
+            xr = raw.tile([P, PACK, D], BF16, name="xr")
+            nc.sync.dma_start(out=xr[:], in_=xf[rows, :].rearrange("(p j) w -> p j w", j=PACK))
+            gr = raw.tile([P, PACK, O], BF16, name="gr")
+            nc.sync.dma_start(out=gr[:], in_=gf[rows, :].rearrange("(p j) w -> p j w", j=PACK))
+            x_raw[c] = xr
+            g_raw[c] = gr
+
+        def regroup(copy, dst, src, lo, hi):
+            copy(
+                out=dst[:, lo:hi, :].rearrange("p (c i) t -> p c t i", i=RUN),
+                in_=src[:, :, lo:hi].rearrange("p t (c i) -> p c t i", i=RUN),
+            )
+
+        def quantise(dst, grouped, lo, hi, fmt):
+            codes, scales = dst
+            nc.vector.quantize_mx(
+                out=codes[:, lo:hi].bitcast(fmt),
+                scales=scales[:, lo:hi],
+                in_=grouped[:, lo:hi, :].rearrange("p w t -> p (w t)"),
+            )
+
+        def passes(c):
+            xq, xs = x_cod[c]
+            gq, gs = g_cod[c]
+            for n in range(N_TILES):
+                for m in range(M_TILES):
+                    nc.tensor.matmul_mx(
+                        out=acc[(m, n)][:],
+                        lhsT=gq[:, m * P : (m + 1) * P].bitcast(E5M2X4),
+                        lhsT_scale=gs[:, m * P : (m + 1) * P],
+                        rhs=xq[:, n * N_TILE : (n + 1) * N_TILE].bitcast(E4M3X4),
+                        rhs_scale=xs[:, n * N_TILE : (n + 1) * N_TILE],
+                        start=(c == 0),
+                        stop=(c == CHUNKS - 1),
+                    )
+
+        for c in range(RAW_BUFS):
+            load(c)
+
+        for c in range(CHUNKS + 1):
+            if c < CHUNKS:
+                xg = grp.tile([P, D, PACK], BF16, name="xg", align_bytes=64)
+                gg = grp.tile([P, O, PACK], BF16, name="gg", align_bytes=64)
+                x_grp[c] = xg
+                g_grp[c] = gg
+                regroup(nc.scalar.copy, xg, x_raw[c], 0, SX)
+                regroup(nc.vector.tensor_copy, xg, x_raw[c], SX, D)
+            if c >= 1:
+                gq = cod.tile([P, O], U32, name="gq", align_bytes=64)
+                gs = cod.tile([P, O], U8, name="gs", align_bytes=64)
+                g_cod[c - 1] = (gq, gs)
+                quantise(g_cod[c - 1], g_grp[c - 1], 0, O, E5M2X4)
+            if c < CHUNKS:
+                regroup(nc.vector.tensor_copy, g_grp[c], g_raw[c], 0, O)
+                if c + RAW_BUFS < CHUNKS:
+                    load(c + RAW_BUFS)
+            if c >= 1:
+                xq = cod.tile([P, D], U32, name="xq", align_bytes=64)
+                xs = cod.tile([P, D], U8, name="xs", align_bytes=64)
+                x_cod[c - 1] = (xq, xs)
+                for n in range(N_TILES):
+                    quantise(x_cod[c - 1], x_grp[c - 1], n * N_TILE, (n + 1) * N_TILE, E4M3X4)
+                passes(c - 1)
+
+        turn = 0
+        for n in range(N_TILES):
+            for m in range(M_TILES):
+                ot = res.tile([P, N_TILE], F32, name="ot")
+                if turn % 2 == 0:
+                    nc.scalar.copy(out=ot[:], in_=acc[(m, n)][:])
+                else:
+                    nc.vector.tensor_copy(out=ot[:], in_=acc[(m, n)][:])
+                turn += 1
+                nc.sync.dma_start(
+                    out=out[m * P : (m + 1) * P, n * N_TILE : (n + 1) * N_TILE], in_=ot[:]
+                )

@@ -17,6 +17,7 @@ D = 1024
 O = 512
 N_TILE = 512
 CHUNKS = T // K_PASS
+LAST = CHUNKS - 1
 M_TILES = O // P
 N_TILES = D // N_TILE
 
@@ -24,7 +25,8 @@ FLOPS = 2 * T * O * D
 BYTES = 2 * T * D + 2 * T * O + 4 * O * D
 
 RAW_BUFS = 8
-SX = 768
+SX = 528
+SG = 264
 RUN = 4
 
 
@@ -62,6 +64,20 @@ def tile_fakequantlinear_t_kernel(tc, x, weight, bias, grad_out, out):
             x_raw[c] = xr
             g_raw[c] = gr
 
+        def open_chunk(c):
+            x_grp[c] = grp.tile([P, D, PACK], BF16, name="xg", align_bytes=64)
+            g_grp[c] = grp.tile([P, O, PACK], BF16, name="gg", align_bytes=64)
+
+        def open_x_codes(c):
+            xq = cod.tile([P, D], U32, name="xq", align_bytes=64)
+            xs = cod.tile([P, D], U8, name="xs", align_bytes=64)
+            x_cod[c] = (xq, xs)
+
+        def open_g_codes(c):
+            gq = cod.tile([P, O], U32, name="gq", align_bytes=64)
+            gs = cod.tile([P, O], U8, name="gs", align_bytes=64)
+            g_cod[c] = (gq, gs)
+
         def regroup(copy, dst, src, lo, hi):
             copy(
                 out=dst[:, lo:hi, :].rearrange("p (c i) t -> p c t i", i=RUN),
@@ -76,58 +92,83 @@ def tile_fakequantlinear_t_kernel(tc, x, weight, bias, grad_out, out):
                 in_=grouped[:, lo:hi, :].rearrange("p w t -> p (w t)"),
             )
 
-        def passes(c):
+        def one_pass(c, m, n):
             xq, xs = x_cod[c]
             gq, gs = g_cod[c]
+            nc.tensor.matmul_mx(
+                out=acc[(m, n)][:],
+                lhsT=gq[:, m * P : (m + 1) * P].bitcast(E5M2X4),
+                lhsT_scale=gs[:, m * P : (m + 1) * P],
+                rhs=xq[:, n * N_TILE : (n + 1) * N_TILE].bitcast(E4M3X4),
+                rhs_scale=xs[:, n * N_TILE : (n + 1) * N_TILE],
+                start=(c == 0),
+                stop=(c == LAST),
+            )
+
+        def passes(c):
             for n in range(N_TILES):
                 for m in range(M_TILES):
-                    nc.tensor.matmul_mx(
-                        out=acc[(m, n)][:],
-                        lhsT=gq[:, m * P : (m + 1) * P].bitcast(E5M2X4),
-                        lhsT_scale=gs[:, m * P : (m + 1) * P],
-                        rhs=xq[:, n * N_TILE : (n + 1) * N_TILE].bitcast(E4M3X4),
-                        rhs_scale=xs[:, n * N_TILE : (n + 1) * N_TILE],
-                        start=(c == 0),
-                        stop=(c == CHUNKS - 1),
-                    )
+                    one_pass(c, m, n)
+
+        def store(copy, m, n):
+            ot = res.tile([P, N_TILE], F32, name="ot")
+            copy(out=ot[:], in_=acc[(m, n)][:])
+            nc.sync.dma_start(
+                out=out[m * P : (m + 1) * P, n * N_TILE : (n + 1) * N_TILE], in_=ot[:]
+            )
+
+        s_copy = nc.scalar.copy
+        v_copy = nc.vector.tensor_copy
 
         for c in range(RAW_BUFS):
             load(c)
 
-        for c in range(CHUNKS + 1):
-            if c < CHUNKS:
-                xg = grp.tile([P, D, PACK], BF16, name="xg", align_bytes=64)
-                gg = grp.tile([P, O, PACK], BF16, name="gg", align_bytes=64)
-                x_grp[c] = xg
-                g_grp[c] = gg
-                regroup(nc.scalar.copy, xg, x_raw[c], 0, SX)
-                regroup(nc.vector.tensor_copy, xg, x_raw[c], SX, D)
+        for c in range(LAST):
+            open_chunk(c)
+            regroup(s_copy, x_grp[c], x_raw[c], 0, SX)
+            regroup(v_copy, x_grp[c], x_raw[c], SX, D)
             if c >= 1:
-                gq = cod.tile([P, O], U32, name="gq", align_bytes=64)
-                gs = cod.tile([P, O], U8, name="gs", align_bytes=64)
-                g_cod[c - 1] = (gq, gs)
+                open_g_codes(c - 1)
                 quantise(g_cod[c - 1], g_grp[c - 1], 0, O, E5M2X4)
-            if c < CHUNKS:
-                regroup(nc.vector.tensor_copy, g_grp[c], g_raw[c], 0, O)
-                if c + RAW_BUFS < CHUNKS:
-                    load(c + RAW_BUFS)
-            if c >= 1:
-                xq = cod.tile([P, D], U32, name="xq", align_bytes=64)
-                xs = cod.tile([P, D], U8, name="xs", align_bytes=64)
-                x_cod[c - 1] = (xq, xs)
-                for n in range(N_TILES):
-                    quantise(x_cod[c - 1], x_grp[c - 1], n * N_TILE, (n + 1) * N_TILE, E4M3X4)
                 passes(c - 1)
+            regroup(s_copy, g_grp[c], g_raw[c], 0, SG)
+            regroup(v_copy, g_grp[c], g_raw[c], SG, O)
+            open_x_codes(c)
+            quantise(x_cod[c], x_grp[c], 0, D, E4M3X4)
+            if c + RAW_BUFS < CHUNKS:
+                load(c + RAW_BUFS)
 
-        turn = 0
-        for n in range(N_TILES):
-            for m in range(M_TILES):
-                ot = res.tile([P, N_TILE], F32, name="ot")
-                if turn % 2 == 0:
-                    nc.scalar.copy(out=ot[:], in_=acc[(m, n)][:])
-                else:
-                    nc.vector.tensor_copy(out=ot[:], in_=acc[(m, n)][:])
-                turn += 1
-                nc.sync.dma_start(
-                    out=out[m * P : (m + 1) * P, n * N_TILE : (n + 1) * N_TILE], in_=ot[:]
-                )
+        c = LAST
+        open_chunk(c)
+        open_x_codes(c)
+        open_g_codes(c - 1)
+        regroup(s_copy, x_grp[c], x_raw[c], 0, 256)
+        quantise(g_cod[c - 1], g_grp[c - 1], 0, O, E5M2X4)
+        open_g_codes(c)
+        regroup(v_copy, x_grp[c], x_raw[c], 256, 512)
+        regroup(s_copy, g_grp[c], g_raw[c], 0, 256)
+        quantise(x_cod[c], x_grp[c], 0, 512, E4M3X4)
+        regroup(v_copy, g_grp[c], g_raw[c], 256, 512)
+        quantise(g_cod[c], g_grp[c], 0, 256, E5M2X4)
+        regroup(s_copy, x_grp[c], x_raw[c], 512, 768)
+        regroup(v_copy, x_grp[c], x_raw[c], 768, 1024)
+        quantise(g_cod[c], g_grp[c], 256, 512, E5M2X4)
+        quantise(x_cod[c], x_grp[c], 512, 1024, E4M3X4)
+
+        for m, n in ((0, 0), (1, 0), (2, 0), (3, 0), (0, 1), (1, 1)):
+            one_pass(c - 1, m, n)
+        for m, n in ((0, 0), (1, 0)):
+            one_pass(c, m, n)
+        for m, n in ((2, 1), (3, 1)):
+            one_pass(c - 1, m, n)
+        for m, n in ((2, 0), (3, 0), (0, 1), (1, 1), (2, 1), (3, 1)):
+            one_pass(c, m, n)
+
+        store(s_copy, 0, 0)
+        store(s_copy, 1, 0)
+        store(s_copy, 2, 0)
+        store(v_copy, 3, 0)
+        store(s_copy, 0, 1)
+        store(v_copy, 1, 1)
+        store(s_copy, 2, 1)
+        store(v_copy, 3, 1)

@@ -25,8 +25,8 @@ FLOPS = 2 * T * O * D
 BYTES = 2 * T * D + 2 * T * O + 4 * O * D
 
 RAW_BUFS = 8
-SX = 528
-SG = 264
+SX = 512
+SG = 256
 RUN = 4
 
 

@@ -25,8 +25,8 @@ FLOPS = 2 * T * O * D
 BYTES = 2 * T * D + 2 * T * O + 4 * O * D
 
 RAW_BUFS = 8
-SX = 512
-SG = 256
+SX = 256
+SG = 512
 RUN = 4
 
 
@@ -132,7 +132,6 @@ def tile_fakequantlinear_t_kernel(tc, x, weight, bias, grad_out, out):
                 quantise(g_cod[c - 1], g_grp[c - 1], 0, O, E5M2X4)
                 passes(c - 1)
             regroup(s_copy, g_grp[c], g_raw[c], 0, SG)
-            regroup(v_copy, g_grp[c], g_raw[c], SG, O)
             open_x_codes(c)
             quantise(x_cod[c], x_grp[c], 0, D, E4M3X4)
             if c + RAW_BUFS < CHUNKS:

@@ -27,7 +27,7 @@ BYTES = 2 * T * D + 2 * T * O + 4 * O * D
 RAW_BUFS = 8
 SX = 256
 SG = 512
-RUN = 4
+RUN = 8
 
 
 def tile_fakequantlinear_t_kernel(tc, x, weight, bias, grad_out, out):

@@ -28,6 +28,7 @@ RAW_BUFS = 8
 SX = 256
 SG = 512
 RUN = 8
+SE = 224
 
 
 def tile_fakequantlinear_t_kernel(tc, x, weight, bias, grad_out, out):
@@ -123,7 +124,7 @@ def tile_fakequantlinear_t_kernel(tc, x, weight, bias, grad_out, out):
         for c in range(RAW_BUFS):
             load(c)
 
-        for c in range(LAST):
+        for c in range(LAST - 1):
             open_chunk(c)
             regroup(s_copy, x_grp[c], x_raw[c], 0, SX)
             regroup(v_copy, x_grp[c], x_raw[c], SX, D)
@@ -137,36 +138,45 @@ def tile_fakequantlinear_t_kernel(tc, x, weight, bias, grad_out, out):
             if c + RAW_BUFS < CHUNKS:
                 load(c + RAW_BUFS)
 
-        c = LAST
-        open_chunk(c)
-        open_x_codes(c)
-        open_g_codes(c - 1)
-        regroup(s_copy, x_grp[c], x_raw[c], 0, 256)
-        quantise(g_cod[c - 1], g_grp[c - 1], 0, O, E5M2X4)
-        open_g_codes(c)
-        regroup(v_copy, x_grp[c], x_raw[c], 256, 512)
-        regroup(s_copy, g_grp[c], g_raw[c], 0, 256)
-        quantise(x_cod[c], x_grp[c], 0, 512, E4M3X4)
-        regroup(v_copy, g_grp[c], g_raw[c], 256, 512)
-        quantise(g_cod[c], g_grp[c], 0, 256, E5M2X4)
-        regroup(s_copy, x_grp[c], x_raw[c], 512, 768)
-        regroup(v_copy, x_grp[c], x_raw[c], 768, 1024)
-        quantise(g_cod[c], g_grp[c], 256, 512, E5M2X4)
-        quantise(x_cod[c], x_grp[c], 512, 1024, E4M3X4)
-
-        for m, n in ((0, 0), (1, 0), (2, 0), (3, 0), (0, 1), (1, 1)):
-            one_pass(c - 1, m, n)
-        for m, n in ((0, 0), (1, 0)):
-            one_pass(c, m, n)
-        for m, n in ((2, 1), (3, 1)):
-            one_pass(c - 1, m, n)
-        for m, n in ((2, 0), (3, 0), (0, 1), (1, 1), (2, 1), (3, 1)):
-            one_pass(c, m, n)
-
-        store(s_copy, 0, 0)
-        store(s_copy, 1, 0)
-        store(s_copy, 2, 0)
-        store(v_copy, 3, 0)
+        a = LAST - 1
+        b = LAST
+        open_chunk(a)
+        open_chunk(b)
+        open_g_codes(a - 1)
+        open_x_codes(a)
+        open_g_codes(a)
+        open_x_codes(b)
+        open_g_codes(b)
+        regroup(s_copy, g_grp[a], g_raw[a], 0, O)
+        regroup(v_copy, x_grp[a], x_raw[a], 0, N_TILE)
+        quantise(g_cod[a - 1], g_grp[a - 1], 0, O, E5M2X4)
+        passes(a - 1)
+        regroup(s_copy, g_grp[b], g_raw[b], 0, O)
+        regroup(v_copy, x_grp[b], x_raw[b], 0, N_TILE)
+        quantise(x_cod[a], x_grp[a], 0, N_TILE, E4M3X4)
+        quantise(g_cod[a], g_grp[a], 0, O, E5M2X4)
+        for m in range(M_TILES):
+            one_pass(a, m, 0)
+        quantise(x_cod[b], x_grp[b], 0, N_TILE, E4M3X4)
+        quantise(g_cod[b], g_grp[b], 0, O, E5M2X4)
+        for m in range(M_TILES):
+            one_pass(b, m, 0)
+        regroup(s_copy, x_grp[a], x_raw[a], N_TILE, N_TILE + SE)
+        regroup(s_copy, x_grp[b], x_raw[b], N_TILE, N_TILE + SE)
+        regroup(v_copy, x_grp[a], x_raw[a], N_TILE + SE, D)
+        regroup(v_copy, x_grp[b], x_raw[b], N_TILE + SE, D)
+        for m in range(M_TILES):
+            store(s_copy, m, 0)
+        quantise(x_cod[a], x_grp[a], N_TILE, D, E4M3X4)
+        quantise(x_cod[b], x_grp[b], N_TILE, D, E4M3X4)
+        one_pass(a, 0, 1)
+        one_pass(a, 1, 1)
+        one_pass(b, 0, 1)
+        one_pass(b, 1, 1)
+        one_pass(a, 2, 1)
+        one_pass(b, 2, 1)
+        one_pass(a, 3, 1)
+        one_pass(b, 3, 1)
         store(s_copy, 0, 1)
         store(v_copy, 1, 1)
         store(s_copy, 2, 1)

@@ -28,7 +28,6 @@ RAW_BUFS = 8
 SX = 256
 SG = 512
 RUN = 8
-SE = 224
 
 
 def tile_fakequantlinear_t_kernel(tc, x, weight, bias, grad_out, out):
@@ -40,6 +39,7 @@ def tile_fakequantlinear_t_kernel(tc, x, weight, bias, grad_out, out):
         raw = ctx.enter_context(tc.tile_pool(name="raw", bufs=RAW_BUFS))
         grp = ctx.enter_context(tc.tile_pool(name="grp", bufs=3))
         cod = ctx.enter_context(tc.tile_pool(name="cod", bufs=3))
+        fin = ctx.enter_context(tc.tile_pool(name="fin", bufs=1))
         res = ctx.enter_context(tc.tile_pool(name="res", bufs=M_TILES * N_TILES))
         psum = ctx.enter_context(tc.psum_pool(name="psum", bufs=1))
         ctx.enter_context(tc.manual_schedule())
@@ -65,6 +65,21 @@ def tile_fakequantlinear_t_kernel(tc, x, weight, bias, grad_out, out):
             x_raw[c] = xr
             g_raw[c] = gr
 
+        def load_end():
+            for c in (LAST - 1, LAST):
+                rows = slice(c * K_PASS, (c + 1) * K_PASS)
+                gr = fin.tile([P, PACK, O], BF16, name="gr%d" % c)
+                nc.sync.dma_start(out=gr[:], in_=gf[rows, :].rearrange("(p j) w -> p j w", j=PACK))
+                g_raw[c] = gr
+                xr = fin.tile([P, PACK, N_TILE], BF16, name="xr%d0" % c)
+                nc.sync.dma_start(out=xr[:], in_=xf[rows, 0:N_TILE].rearrange("(p j) w -> p j w", j=PACK))
+                x_raw[(c, 0)] = xr
+            for c in (LAST - 1, LAST):
+                rows = slice(c * K_PASS, (c + 1) * K_PASS)
+                xr = fin.tile([P, PACK, N_TILE], BF16, name="xr%d1" % c)
+                nc.sync.dma_start(out=xr[:], in_=xf[rows, N_TILE:D].rearrange("(p j) w -> p j w", j=PACK))
+                x_raw[(c, 1)] = xr
+
         def open_chunk(c):
             x_grp[c] = grp.tile([P, D, PACK], BF16, name="xg", align_bytes=64)
             g_grp[c] = grp.tile([P, O, PACK], BF16, name="gg", align_bytes=64)
@@ -79,10 +94,10 @@ def tile_fakequantlinear_t_kernel(tc, x, weight, bias, grad_out, out):
             gs = cod.tile([P, O], U8, name="gs", align_bytes=64)
             g_cod[c] = (gq, gs)
 
-        def regroup(copy, dst, src, lo, hi):
+        def regroup(copy, dst, src, lo, hi, first=0):
             copy(
                 out=dst[:, lo:hi, :].rearrange("p (c i) t -> p c t i", i=RUN),
-                in_=src[:, :, lo:hi].rearrange("p t (c i) -> p c t i", i=RUN),
+                in_=src[:, :, lo - first : hi - first].rearrange("p t (c i) -> p c t i", i=RUN),
             )
 
         def quantise(dst, grouped, lo, hi, fmt):
@@ -135,8 +150,10 @@ def tile_fakequantlinear_t_kernel(tc, x, weight, bias, grad_out, out):
             regroup(s_copy, g_grp[c], g_raw[c], 0, SG)
             open_x_codes(c)
             quantise(x_cod[c], x_grp[c], 0, D, E4M3X4)
-            if c + RAW_BUFS < CHUNKS:
+            if c + RAW_BUFS < LAST - 1:
                 load(c + RAW_BUFS)
+            if c + RAW_BUFS == LAST - 2:
+                load_end()
 
         a = LAST - 1
         b = LAST
@@ -147,26 +164,28 @@ def tile_fakequantlinear_t_kernel(tc, x, weight, bias, grad_out, out):
         open_g_codes(a)
         open_x_codes(b)
         open_g_codes(b)
-        regroup(s_copy, g_grp[a], g_raw[a], 0, O)
-        regroup(v_copy, x_grp[a], x_raw[a], 0, N_TILE)
         quantise(g_cod[a - 1], g_grp[a - 1], 0, O, E5M2X4)
         passes(a - 1)
-        regroup(s_copy, g_grp[b], g_raw[b], 0, O)
-        regroup(v_copy, x_grp[b], x_raw[b], 0, N_TILE)
-        quantise(x_cod[a], x_grp[a], 0, N_TILE, E4M3X4)
+        regroup(s_copy, g_grp[a], g_raw[a], 0, O)
+        regroup(v_copy, x_grp[a], x_raw[(a, 0)], 0, N_TILE)
         quantise(g_cod[a], g_grp[a], 0, O, E5M2X4)
+        quantise(x_cod[a], x_grp[a], 0, N_TILE, E4M3X4)
         for m in range(M_TILES):
             one_pass(a, m, 0)
-        quantise(x_cod[b], x_grp[b], 0, N_TILE, E4M3X4)
+        regroup(s_copy, g_grp[b], g_raw[b], 0, O)
+        regroup(v_copy, x_grp[b], x_raw[(b, 0)], 0, N_TILE)
         quantise(g_cod[b], g_grp[b], 0, O, E5M2X4)
+        quantise(x_cod[b], x_grp[b], 0, N_TILE, E4M3X4)
         for m in range(M_TILES):
             one_pass(b, m, 0)
-        regroup(s_copy, x_grp[a], x_raw[a], N_TILE, N_TILE + SE)
-        regroup(s_copy, x_grp[b], x_raw[b], N_TILE, N_TILE + SE)
-        regroup(v_copy, x_grp[a], x_raw[a], N_TILE + SE, D)
-        regroup(v_copy, x_grp[b], x_raw[b], N_TILE + SE, D)
-        for m in range(M_TILES):
-            store(s_copy, m, 0)
+        regroup(s_copy, x_grp[a], x_raw[(a, 1)], N_TILE, N_TILE + 256, N_TILE)
+        regroup(v_copy, x_grp[a], x_raw[(a, 1)], N_TILE + 256, D, N_TILE)
+        regroup(s_copy, x_grp[b], x_raw[(b, 1)], N_TILE, N_TILE + 128, N_TILE)
+        regroup(v_copy, x_grp[b], x_raw[(b, 1)], N_TILE + 128, D, N_TILE)
+        store(s_copy, 0, 0)
+        store(s_copy, 1, 0)
+        store(s_copy, 2, 0)
+        store(s_copy, 3, 0)
         quantise(x_cod[a], x_grp[a], N_TILE, D, E4M3X4)
         quantise(x_cod[b], x_grp[b], N_TILE, D, E4M3X4)
         one_pass(a, 0, 1)

from contextlib import ExitStack

import concourse.mybir as mybir

BF16 = mybir.dt.bfloat16
F32 = mybir.dt.float32
U32 = mybir.dt.uint32
U8 = mybir.dt.uint8
E4M3X4 = mybir.dt.float8_e4m3fn_x4
E5M2X4 = mybir.dt.float8_e5m2_x4

P = 128
PACK = 4
K_PASS = P * PACK
T = 4 * 2048
D = 1024
O = 512
N_TILE = 512
CHUNKS = T // K_PASS
LAST = CHUNKS - 1
M_TILES = O // P
N_TILES = D // N_TILE

FLOPS = 2 * T * O * D
BYTES = 2 * T * D + 2 * T * O + 4 * O * D

RAW_BUFS = 8
SX = 256
SG = 512
RUN = 8


def tile_fakequantlinear_t_kernel(tc, x, weight, bias, grad_out, out):
    nc = tc.nc
    xf = x.rearrange("b s d -> (b s) d")
    gf = grad_out.rearrange("b s o -> (b s) o")

    with ExitStack() as ctx:
        raw = ctx.enter_context(tc.tile_pool(name="raw", bufs=RAW_BUFS))
        grp = ctx.enter_context(tc.tile_pool(name="grp", bufs=3))
        cod = ctx.enter_context(tc.tile_pool(name="cod", bufs=3))
        fin = ctx.enter_context(tc.tile_pool(name="fin", bufs=1))
        res = ctx.enter_context(tc.tile_pool(name="res", bufs=M_TILES * N_TILES))
        psum = ctx.enter_context(tc.psum_pool(name="psum", bufs=1))
        ctx.enter_context(tc.manual_schedule())

        acc = {}
        for m in range(M_TILES):
            for n in range(N_TILES):
                acc[(m, n)] = psum.tile([P, N_TILE], F32, name="acc%d%d" % (m, n))

        x_raw = {}
        g_raw = {}
        x_grp = {}
        g_grp = {}
        x_cod = {}
        g_cod = {}

        def load(c):
            rows = slice(c * K_PASS, (c + 1) * K_PASS)
            xr = raw.tile([P, PACK, D], BF16, name="xr")
            nc.sync.dma_start(out=xr[:], in_=xf[rows, :].rearrange("(p j) w -> p j w", j=PACK))
            gr = raw.tile([P, PACK, O], BF16, name="gr")
            nc.sync.dma_start(out=gr[:], in_=gf[rows, :].rearrange("(p j) w -> p j w", j=PACK))
            x_raw[c] = xr
            g_raw[c] = gr

        def load_end():
            for c in (LAST - 1, LAST):
                rows = slice(c * K_PASS, (c + 1) * K_PASS)
                gr = fin.tile([P, PACK, O], BF16, name="gr%d" % c)
                nc.sync.dma_start(out=gr[:], in_=gf[rows, :].rearrange("(p j) w -> p j w", j=PACK))
                g_raw[c] = gr
                xr = fin.tile([P, PACK, N_TILE], BF16, name="xr%d0" % c)
                nc.sync.dma_start(out=xr[:], in_=xf[rows, 0:N_TILE].rearrange("(p j) w -> p j w", j=PACK))
                x_raw[(c, 0)] = xr
            for c in (LAST - 1, LAST):
                rows = slice(c * K_PASS, (c + 1) * K_PASS)
                xr = fin.tile([P, PACK, N_TILE], BF16, name="xr%d1" % c)
                nc.sync.dma_start(out=xr[:], in_=xf[rows, N_TILE:D].rearrange("(p j) w -> p j w", j=PACK))
                x_raw[(c, 1)] = xr

        def open_chunk(c):
            x_grp[c] = grp.tile([P, D, PACK], BF16, name="xg", align_bytes=64)
            g_grp[c] = grp.tile([P, O, PACK], BF16, name="gg", align_bytes=64)

        def open_x_codes(c):
            xq = cod.tile([P, D], U32, name="xq", align_bytes=64)
            xs = cod.tile([P, D], U8, name="xs", align_bytes=64)
            x_cod[c] = (xq, xs)

        def open_g_codes(c):
            gq = cod.tile([P, O], U32, name="gq", align_bytes=64)
            gs = cod.tile([P, O], U8, name="gs", align_bytes=64)
            g_cod[c] = (gq, gs)

        def regroup(copy, dst, src, lo, hi, first=0):
            copy(
                out=dst[:, lo:hi, :].rearrange("p (c i) t -> p c t i", i=RUN),
                in_=src[:, :, lo - first : hi - first].rearrange("p t (c i) -> p c t i", i=RUN),
            )

        def quantise(dst, grouped, lo, hi, fmt):
            codes, scales = dst
            nc.vector.quantize_mx(
                out=codes[:, lo:hi].bitcast(fmt),
                scales=scales[:, lo:hi],
                in_=grouped[:, lo:hi, :].rearrange("p w t -> p (w t)"),
            )

        def one_pass(c, m, n):
            xq, xs = x_cod[c]
            gq, gs = g_cod[c]
            nc.tensor.matmul_mx(
                out=acc[(m, n)][:],
                lhsT=gq[:, m * P : (m + 1) * P].bitcast(E5M2X4),
                lhsT_scale=gs[:, m * P : (m + 1) * P],
                rhs=xq[:, n * N_TILE : (n + 1) * N_TILE].bitcast(E4M3X4),
                rhs_scale=xs[:, n * N_TILE : (n + 1) * N_TILE],
                start=(c == 0),
                stop=(c == LAST),
            )

        def passes(c):
            for n in range(N_TILES):
                for m in range(M_TILES):
                    one_pass(c, m, n)

        def store(copy, m, n):
            ot = res.tile([P, N_TILE], F32, name="ot")
            copy(out=ot[:], in_=acc[(m, n)][:])
            nc.sync.dma_start(
                out=out[m * P : (m + 1) * P, n * N_TILE : (n + 1) * N_TILE], in_=ot[:]
            )

        s_copy = nc.scalar.copy
        v_copy = nc.vector.tensor_copy

        for c in range(RAW_BUFS):
            load(c)

        for c in range(LAST - 1):
            open_chunk(c)
            regroup(s_copy, x_grp[c], x_raw[c], 0, SX)
            regroup(v_copy, x_grp[c], x_raw[c], SX, D)
            if c >= 1:
                open_g_codes(c - 1)
                quantise(g_cod[c - 1], g_grp[c - 1], 0, O, E5M2X4)
                passes(c - 1)
            regroup(s_copy, g_grp[c], g_raw[c], 0, SG)
            open_x_codes(c)
            quantise(x_cod[c], x_grp[c], 0, D, E4M3X4)
            if c + RAW_BUFS < LAST - 1:
                load(c + RAW_BUFS)
            if c + RAW_BUFS == LAST - 2:
                load_end()

        a = LAST - 1
        b = LAST
        open_chunk(a)
        open_chunk(b)
        open_g_codes(a - 1)
        open_x_codes(a)
        open_g_codes(a)
        open_x_codes(b)
        open_g_codes(b)
        quantise(g_cod[a - 1], g_grp[a - 1], 0, O, E5M2X4)
        passes(a - 1)
        regroup(s_copy, g_grp[a], g_raw[a], 0, O)
        regroup(v_copy, x_grp[a], x_raw[(a, 0)], 0, N_TILE)
        quantise(g_cod[a], g_grp[a], 0, O, E5M2X4)
        quantise(x_cod[a], x_grp[a], 0, N_TILE, E4M3X4)
        for m in range(M_TILES):
            one_pass(a, m, 0)
        regroup(s_copy, g_grp[b], g_raw[b], 0, O)
        regroup(v_copy, x_grp[b], x_raw[(b, 0)], 0, N_TILE)
        quantise(g_cod[b], g_grp[b], 0, O, E5M2X4)
        quantise(x_cod[b], x_grp[b], 0, N_TILE, E4M3X4)
        for m in range(M_TILES):
            one_pass(b, m, 0)
        regroup(s_copy, x_grp[a], x_raw[(a, 1)], N_TILE, N_TILE + 256, N_TILE)
        regroup(v_copy, x_grp[a], x_raw[(a, 1)], N_TILE + 256, D, N_TILE)
        regroup(s_copy, x_grp[b], x_raw[(b, 1)], N_TILE, N_TILE + 128, N_TILE)
        regroup(v_copy, x_grp[b], x_raw[(b, 1)], N_TILE + 128, D, N_TILE)
        store(s_copy, 0, 0)
        store(s_copy, 1, 0)
        store(s_copy, 2, 0)
        store(s_copy, 3, 0)
        quantise(x_cod[a], x_grp[a], N_TILE, D, E4M3X4)
        quantise(x_cod[b], x_grp[b], N_TILE, D, E4M3X4)
        one_pass(a, 0, 1)
        one_pass(a, 1, 1)
        one_pass(b, 0, 1)
        one_pass(b, 1, 1)
        one_pass(a, 2, 1)
        one_pass(b, 2, 1)
        one_pass(a, 3, 1)
        one_pass(b, 3, 1)
        store(s_copy, 0, 1)
        store(v_copy, 1, 1)
        store(s_copy, 2, 1)
        store(v_copy, 3, 1)
